import numpy as np
import ml_dtypes


def mxq(x, axis, fmt="e4m3"):
    dtype, down = {"e4m3": (ml_dtypes.float8_e4m3fn, 7), "e5m2": (ml_dtypes.float8_e5m2, 14)}[fmt]
    v = np.moveaxis(np.asarray(x, np.float32).astype(ml_dtypes.bfloat16).astype(np.float64), axis, -1)
    blocks = v.reshape(v.shape[:-1] + (-1, 32))
    amax = np.abs(blocks).max(-1, keepdims=True)
    byte = np.maximum(np.where(amax > 0, np.frexp(amax)[1] - 1 + 127, 0) - down, 1)
    scale = np.exp2(byte - 127.0)
    codes = (blocks / scale).astype(np.float32).astype(dtype).astype(np.float64)
    return np.moveaxis((codes * scale).reshape(v.shape), -1, axis)


WIDE = False


def mx_kscale(k):
    if not WIDE:
        return np.ones(k)
    levels = np.array([18, -18])
    if k % 512:
        return np.exp2(np.random.permutation(np.resize(levels, k // 32))).repeat(32)
    a = np.empty((k // 512, 16))
    for p in range(k // 512):
        a[p, :8] = np.random.permutation(np.resize(levels, 8))
        for g in range(8):
            far = levels[np.abs(levels - a[p, g]) >= 10]
            a[p, g + 8] = far[np.random.randint(len(far))]
    return np.exp2(a.ravel()).repeat(32)


BF16 = ml_dtypes.bfloat16


def bf(x):
    return np.asarray(x, np.float32).astype(BF16)


def f64(x):
    return np.asarray(x).astype(np.float64)


B, S, HID, NH, NKV, HD = 2, 512, 1024, 8, 4, 128
T = B * S
JQ, JK = NH * HD, NKV * HD
EPS = 1e-6


def rstd(u):
    return 1.0 / np.sqrt(np.mean(u * u, axis=-1, keepdims=True) + EPS)


def rotate_half(u):
    u1, u2 = np.split(u, 2, axis=-1)
    return np.concatenate([-u2, u1], axis=-1)


def unrotate_half(u):
    u1, u2 = np.split(u, 2, axis=-1)
    return np.concatenate([u2, -u1], axis=-1)


def rms_back(dn, u, r, w):
    gw = dn * w
    uh = u * r
    return r * (gw - uh * np.mean(gw * uh, axis=-1, keepdims=True))


def setup_inputs():
    s = mx_kscale(T)
    uqk = np.repeat(mx_kscale(512), HD // 32)[:JQ + JK]
    uq, uk = uqk[:JQ], uqk[JQ:]
    uv = mx_kscale(JK)
    pos = np.tile(np.arange(S, dtype=np.float64), B)
    inv_freq = 1.0 / (10000.0 ** (np.arange(0, HD, 2, dtype=np.float64) / HD))
    ang = pos[:, None] * inv_freq[None, :]
    emb = np.concatenate([ang, ang], axis=-1)
    a = 1.0 / np.sqrt(HID)
    x0 = bf(np.random.standard_normal((T, HID)) * 0.5)
    wq0 = bf(np.random.standard_normal((JQ, HID)) * a)
    bq = bf(np.random.standard_normal(JQ) * 0.3)
    wk0 = bf(np.random.standard_normal((JK, HID)) * a)
    bk = bf(np.random.standard_normal(JK) * 0.3)
    wv0 = bf(np.random.standard_normal((JK, HID)) * 2.0 * a)
    bv = bf(np.random.standard_normal(JK) * 0.3)
    q_norm_w = bf(1.0 + 0.1 * np.random.standard_normal(HD))
    k_norm_w = bf(1.0 + 0.1 * np.random.standard_normal(HD))
    ln1_w = bf(1.0 + 0.1 * np.random.standard_normal(HID))
    r1 = rstd(f64(x0))
    h0 = f64(x0) * r1 * f64(ln1_w)
    q_pre = h0 @ f64(wq0).T + f64(bq)
    k_pre = h0 @ f64(wk0).T + f64(bk)
    g0 = np.random.standard_normal((T, NH, HD)) * np.exp2(np.random.randint(-6, 1, (T, 1, 1)))
    g1 = np.random.standard_normal((T, NKV, HD)) * np.exp2(np.random.randint(-6, 1, (T, 1, 1)))
    g2 = np.random.standard_normal((T, NKV, HD)) * np.exp2(np.random.randint(-6, 1, (T, 1, 1)))
    st = s[:, None, None]
    return {"x": bf(f64(x0) * s[:, None]),
            "cos": bf(np.cos(emb)),
            "sin": bf(np.sin(emb)),
            "wq": bf(f64(wq0) / uq[:, None]),
            "bq": bq,
            "wk": bf(f64(wk0) / uk[:, None]),
            "bk": bk,
            "wv": bf(f64(wv0) / uv[:, None]),
            "bv": bv,
            "q_norm_w": q_norm_w,
            "k_norm_w": k_norm_w,
            "ln1_w": ln1_w,
            "q_pre": np.asarray(q_pre, np.float32),
            "k_pre": np.asarray(k_pre, np.float32),
            "x_rstd": np.asarray(r1, np.float32),
            "grad_0": bf(g0 / st * uq.reshape(1, NH, HD)),
            "grad_1": bf(g1 / st * uk.reshape(1, NKV, HD)),
            "grad_2": bf(g2 / st * uv.reshape(1, NKV, HD))}


def reference(x, cos, sin, wq, bq, wk, bk, wv, bv, q_norm_w, k_norm_w, ln1_w, q_pre, k_pre, x_rstd, grad_0, grad_1, grad_2):
    c, sn = f64(cos)[:, None, :], f64(sin)[:, None, :]
    g0, g1 = f64(grad_0), f64(grad_1)
    dnq = g0 * c + unrotate_half(g0 * sn)
    dnk = g1 * c + unrotate_half(g1 * sn)
    uq = f64(q_pre).reshape(T, NH, HD)
    uk = f64(k_pre).reshape(T, NKV, HD)
    dzq = rms_back(dnq, uq, rstd(uq), f64(q_norm_w)).reshape(T, JQ)
    dzk = rms_back(dnk, uk, rstd(uk), f64(k_norm_w)).reshape(T, JK)
    dzv = f64(grad_2).reshape(T, JK)
    dz = np.concatenate([dzq, dzk, dzv], axis=1)
    w = np.concatenate([f64(wq), f64(wk), f64(wv)], axis=0)
    r1 = f64(x_rstd)
    h = f64(x) * r1 * f64(ln1_w)
    dh = mxq(dz, 1, "e5m2") @ mxq(w, 0, "e4m3")
    dw = mxq(dz, 0, "e5m2").T @ mxq(h, 0, "e4m3")
    dx = rms_back(dh, f64(x), r1, f64(ln1_w))
    return dx, dw[:JQ], dw[JQ:JQ + JK], dw[JQ + JK:]

from contextlib import ExitStack

import concourse.mybir as mybir
from concourse.masks import make_identity

F32 = mybir.dt.float32
BF16 = mybir.dt.bfloat16
U32 = mybir.dt.uint32
U8 = mybir.dt.uint8
E4 = mybir.dt.float8_e4m3fn_x4
E5 = mybir.dt.float8_e5m2_x4
ALU = mybir.AluOpType
ACT = mybir.ActivationFunctionType

P = 128
T = 1024
HID = 1024
JQ, JK = 1024, 512
JALL = JQ + 2 * JK
HD = 128
EPS = 1e-6
FLOPS = 2 * 2 * T * JALL * HID
BYTES = (2 * T * HID + 4 * T * HD + 2 * JALL * HID + 4 * T * (JQ + JK) + 4 * T + 2 * T * JALL + 4 * T * HID + 4 * JALL * HID)
CH = 512
NCH = 3
NV = 3
HPC = 4
UB, GB = 7, 3
ADD_ENGINE = "g"
CORE = (("cos", 0, ()), ("sin", 0, ()), ("slope", 2, ()), ("add", 1, ()), ("fin", 2, (0,)), ("fin", 2, (1,)), ("flip", 2, ()), ("scale", 1, ()), ("fcopy", 2, ()), ("prod", 1, ()), ("dots", 1, ()), ("qflip", 2, ()))

ORDER = {
    (-1, 0): [("load_cs", (0, )), ("load_u", (0, )), ("spread", ()), ("load_g", (0, )), ("flip_cs", (0, )), ("tables", (0, 0, 0, )), ("load_u", (2, )), ("tables", (0, 0, 1, ))],
    (0, 0): [("sq", (0, )), ("mean", (0, slice(0, 8), )), ("load_u", (1, ))],
    (0, 1): [("sq", (2, )), ("load_g", (1, ))],
    (1, 0): [("load_u", (3, )), ("root", (0, slice(0, 8), )), ("load_g", (2, ))],
    (1, 1): [("sq", (1, ))],
    (1, 3): [("sq", (3, )), ("mean", (0, slice(8, 24), )), ("load_w", (2, )), ("rr", (0, slice(0, 8), )), ("load_x", (0, ))],
    (1, 7): [("tables", (0, 1, 1, ))],
    (1, 9): [("root", (0, slice(8, 24), ))],
    (1, 10): [("wil", (2, (0, 1), ))],
    (2, 0): [("wil", (2, (2, 3), )), ("load_u", (4, )), ("rr", (0, slice(8, 24), ))],
    (2, 1): [("sq", (4, )), ("tables", (0, 1, 0, ))],
    (2, 3): [("load_g", (4, )), ("h", (0, (0,), ))],
    (2, 4): [("load_g", (3, )), ("load_u", (5, ))],
    (2, 7): [("load_w", (1, ))],
    (2, 8): [("sq", (5, ))],
    (2, 9): [("h", (0, (2,), )), ("h", (0, (1,), ))],
    (2, 10): [("h", (0, (3,), )), ("hil", (0, (0,), )), ("wil", (1, (0, 1), ))],
    (2, 11): [("hil", (0, (3,), ))],
    (3, 2): [("load_w", (3, ))],
    (3, 3): [("mean", (1, slice(0, 24), ))],
    (3, 6): [("load_cs", (1, ))],
    (3, 8): [("load_v", (1, ))],
    (3, 9): [("wq", (2, ))],
    (3, 10): [("wil", (1, (2, 3), )), ("load_g", (5, )), ("root", (1, slice(0, 24), ))],
    (4, 0): [("hil", (0, (2,), )), ("load_v", (0, )), ("wil", (3, (0, 1), ))],
    (4, 1): [("load_u", (11, )), ("load_g", (8, ))],
    (4, 2): [("load_x", (1, ))],
    (4, 3): [("rr", (1, slice(0, 24), ))],
    (4, 4): [("load_w", (0, )), ("wil", (3, (2, 3), )), ("hil", (0, (1,), ))],
    (4, 8): [("wq", (1, ))],
    (4, 9): [("ilv", (0, )), ("fl", (0, 0, 3, ))],
    (4, 10): [("flip_cs", (1, )), ("wq", (3, )), ("qh", (0, ))],
    (4, 11): [("fc", (0, 0, 3, ))],
    (5, 0): [("h", (1, (0,), )), ("load_u", (8, )), ("load_u", (6, ))],
    (5, 1): [("wil", (0, (0, 1), ))],
    (5, 2): [("wil", (0, (2, 3), )), ("qf", (0, 0, 3, )), ("tables", (1, 0, 0, ))],
    (5, 5): [("qt", (0, 3, ))],
    (5, 6): [("load_g", (6, ))],
    (5, 9): [("wq", (0, )), ("fl", (0, 1, 3, )), ("load_u", (7, ))],
    (6, 2): [("dh", (0, 0, ))],
    (6, 3): [("sq", (6, )), ("h", (1, (3,), ))],
    (6, 4): [("sq", (7, )), ("sq", (8, )), ("load_g", (7, )), ("fc", (0, 1, 3, ))],
    (6, 7): [("load_u", (10, ))],
    (6, 8): [("load_u", (9, )), ("dxa", (0, 0, ))],
    (6, 9): [("mean", (2, slice(0, 24), )), ("h", (1, (1,), )), ("dxb", (0, 0, )), ("root", (2, slice(0, 24), ))],
    (6, 10): [("rr", (2, slice(0, 24), )), ("il", (0, 0, (0,), )), ("sq", (9, ))],
    (6, 11): [("tables", (1, 0, 1, ))],
    (7, 1): [("ilv", (1, ))],
    (7, 3): [("qf", (0, 1, 3, ))],
    (7, 6): [("il", (0, 0, (1,), ))],
    (7, 9): [("h", (1, (2,), ))],
    (7, 10): [("sq", (11, ))],
    (8, 1): [("tables", (1, 1, 1, )), ("qt", (0, 0, ))],
    (8, 2): [("qt", (1, 3, ))],
    (8, 3): [("dh", (0, 1, ))],
    (8, 4): [("sq", (10, ))],
    (8, 5): [("tables", (1, 1, 0, )), ("hil", (1, (0,), ))],
    (8, 6): [("dxa", (0, 1, ))],
    (8, 9): [("mean", (3, slice(0, 24), ))],
    (8, 11): [("load_g", (9, )), ("il", (0, 1, (0,), )), ("load_g", (10, )), ("il", (0, 1, (1,), ))],
    (9, 0): [("hil", (1, (2,), )), ("dxc", (0, 0, )), ("dh", (0, 2, ))],
    (9, 2): [("il", (0, 2, (0,), )), ("dxb", (0, 1, ))],
    (9, 9): [("load_g", (11, )), ("dxa", (0, 2, ))],
    (10, 0): [("il", (0, 2, (1,), ))],
    (10, 2): [("dxc", (0, 1, ))],
    (10, 3): [("root", (3, slice(0, 24), )), ("hil", (1, (1,), ))],
    (10, 5): [("rr", (3, slice(0, 24), )), ("hil", (1, (3,), ))],
    (10, 7): [("dh", (0, 3, ))],
    (10, 10): [("qh", (1, ))],
    (10, 11): [("dw", (3, 2, 'ss', ))],
    (11, 0): [("dw", (3, 3, 'ss', )), ("dw", (3, 0, 'ss', ))],
    (11, 3): [("qt", (0, 1, )), ("dw", (3, 1, 'ss', )), ("fl", (1, 0, 3, )), ("fc", (1, 0, 3, ))],
    (11, 6): [("dxb", (0, 2, ))],
    (11, 9): [("dxa", (0, 3, )), ("qf", (1, 0, 3, ))],
    (11, 10): [("il", (1, 0, (0,), )), ("dxc", (0, 2, ))],
    (12, 2): [("qt", (0, 2, ))],
    (12, 4): [("il", (1, 0, (1,), )), ("fl", (1, 1, 3, ))],
    (12, 5): [("il", (1, 1, (0,), )), ("dxb", (0, 3, )), ("fc", (1, 1, 3, )), ("dh", (1, 0, ))],
    (12, 6): [("qt", (1, 0, ))],
    (12, 8): [("dxa", (1, 0, ))],
    (12, 9): [("il", (1, 1, (1,), )), ("dxc", (0, 3, )), ("dw", (0, 0, 'ss', )), ("dxb", (1, 0, ))],
    (12, 11): [("qt", (1, 1, ))],
    (13, 2): [("qf", (1, 1, 3, ))],
    (13, 4): [("dh", (1, 1, ))],
    (13, 5): [("dw", (0, 2, 'ss', )), ("dw", (0, 1, 'ss', )), ("dxc", (1, 0, )), ("dxa", (1, 1, )), ("dw", (1, 2, 'ss', ))],
    (13, 11): [("dxb", (1, 1, )), ("dxc", (1, 1, )), ("dw", (1, 0, 'ss', )), ("il", (1, 2, (0,), )), ("il", (1, 2, (1,), )), ("dh", (1, 2, )), ("dxa", (1, 2, )), ("dw", (0, 3, 'ss', )), ("dw", (1, 1, 'ss', )), ("qt", (1, 2, )), ("dxb", (1, 2, )), ("dw", (2, 2, 'vs', )), ("dh", (1, 3, )), ("dxc", (1, 2, )), ("dxa", (1, 3, )), ("dw", (2, 3, 'vs', )), ("dxb", (1, 3, )), ("dw", (1, 3, 'ss', )), ("dw", (2, 0, 'vs', )), ("dxc", (1, 3, )), ("dw", (2, 1, 'vs', ))],
}


def tile_qwen2decoderlayer_pa_v_kernel(
    tc, x, cos, sin, wq, bq, wk, bk, wv, bv, q_norm_w, k_norm_w, ln1_w, q_pre, k_pre, x_rstd, grad_0, grad_1, grad_2,
    out_0, out_1, out_2, out_3,
):
    nc = tc.nc
    with ExitStack() as ctx:
        one = ctx.enter_context(tc.tile_pool(name="one", bufs=1))
        rot = ctx.enter_context(tc.tile_pool(name="rot", bufs=2))
        ps = ctx.enter_context(tc.psum_pool(name="ps", bufs=2))
        ctx.enter_context(tc.manual_schedule())

        ident = one.tile([P, P], BF16, name="ident")
        ident32 = one.tile([P, P], F32, name="ident32")
        ones = one.tile([P, P], BF16, name="ones")
        wrow = one.tile([P, HID + 2 * HD], BF16, name="wrow")
        lnw = one.tile([P, HID], BF16, name="lnw")
        nw = one.tile([P, 2 * HD], F32, name="nw")
        mcos = one.tile([P, 2, HD], BF16, name="mcos")
        msin = one.tile([P, 2, HD], BF16, name="msin")
        r1 = one.tile([P, 8], F32, name="r1")
        r1n = one.tile([P, 8], F32, name="r1n")
        warm = one.tile([P, 1], F32, name="warm")
        junk = one.tile([P, 4, HD], BF16, name="junk")
        junkx = one.tile([P, HID], BF16, name="junkx")
        w_codes = one.tile([P, 4, HID], U32, name="w_codes", align_bytes=64)
        w_scales = one.tile([P, 4, HID], U8, name="w_scales", align_bytes=64)
        h_codes = one.tile([P, 2, HID], U32, name="h_codes", align_bytes=64)
        h_scales = one.tile([P, 2, HID], U8, name="h_scales", align_bytes=64)
        d_codes = one.tile([P, 2, 4, CH], U32, name="d_codes", align_bytes=64)
        d_scales = one.tile([P, 2, 4, CH], U8, name="d_scales", align_bytes=64)

        nc.gpsimd.memset(wrow[:], 0.0)
        nc.vector.memset(ones[:], 1.0)
        nc.vector.memset(warm[:], 1.0)
        make_identity(nc, ident[:])
        nc.scalar.dma_start(out=wrow[0:1, HID:HID + HD], in_=q_norm_w.rearrange("(o d) -> o d", o=1))
        nc.scalar.dma_start(out=wrow[0:1, HID + HD:HID + 2 * HD], in_=k_norm_w.rearrange("(o d) -> o d", o=1))
        nc.scalar.dma_start(out=wrow[0:1, 0:HID], in_=ln1_w.rearrange("(o d) -> o d", o=1))
        nc.scalar.dma_start(out=r1[:].rearrange("p (g j) -> p g j", g=2), in_=x_rstd.rearrange("(g p j) o -> p g (j o)", g=2, j=4))
        nc.scalar.activation(out=warm[:], in_=warm[:], func=ACT.Sqrt)
        nc.vector.tensor_copy(out=ident32[:], in_=ident[:])

        def rows(ap, g):
            return ap.rearrange("(g p j) w -> g p j w", g=2, j=4)[g]

        flat = {0: grad_0.rearrange("t h d -> t (h d)"), 1: grad_1.rearrange("t h d -> t (h d)"), 2: grad_2.rearrange("t h d -> t (h d)")}
        units = [(g, jp, c) for g in range(2) for jp in range(2) for c in range(NCH)]
        cs = {}
        ut = {}
        gt = {}
        gv = {}
        wraw = {}
        xt = {}

        def load_cs(g):
            cs[g] = rot.tile([P, 2, 4, HD], BF16, name="cs", tag="cs", bufs=1)
            nc.sync.dma_start(out=cs[g][:, 0], in_=rows(cos, g))
            nc.sync.dma_start(out=cs[g][:, 1], in_=rows(sin, g))

        def load_u(k):
            g, jp, c = units[k]
            js = slice(2 * jp, 2 * jp + 2)
            u_src = rows(k_pre, g)[:, js] if c == 2 else rows(q_pre, g)[:, js, c * CH:(c + 1) * CH]
            ut[k] = rot.tile([P, 2, CH], F32, name="ut", tag="ut", bufs=UB)
            nc.sync.dma_start(out=ut[k][:], in_=u_src)

        def load_g(k):
            g, jp, c = units[k]
            js = slice(2 * jp, 2 * jp + 2)
            g_src = rows(flat[1], g)[:, js] if c == 2 else rows(flat[0], g)[:, js, c * CH:(c + 1) * CH]
            gt[k] = rot.tile([P, 2, CH], BF16, name="gt", tag="gt", bufs=GB)
            nc.sync.dma_start(out=gt[k][:], in_=g_src)

        def load_v(g):
            gv[g] = rot.tile([P, 4, JK], BF16, name="gv", tag="gv", bufs=2)
            nc.sync.dma_start(out=gv[g][:], in_=rows(flat[2], g))

        def load_w(kp):
            src = (wq[0:512], wq[512:1024], wk, wv)[kp]
            wraw[kp] = rot.tile([P, 4, HID], BF16, name="wraw", tag="big", bufs=5, align_bytes=64)
            nc.sync.dma_start(out=wraw[kp][:], in_=src.rearrange("(p j) n -> p j n", j=4))

        def load_x(g):
            xt[g] = rot.tile([P, 4, HID], BF16, name="xt", tag="xt", bufs=2)
            nc.sync.dma_start(out=xt[g][:], in_=rows(x, g))

        def spread_weights():
            b0 = ps.tile([P, 512], F32, name="b0", tag="mm", bufs=3)
            nc.tensor.matmul(out=b0[:, 0:256], lhsT=ones[:], rhs=wrow[:, HID:HID + 256], start=True, stop=True)
            nc.scalar.copy(out=nw[:], in_=b0[:, 0:256])
            for i in range(2):
                b1 = ps.tile([P, 512], F32, name="b1", tag="mm", bufs=3)
                nc.tensor.matmul(out=b1[:], lhsT=ones[:], rhs=wrow[:, i * 512:(i + 1) * 512], start=True, stop=True)
                nc.scalar.copy(out=lnw[:, i * 512:(i + 1) * 512], in_=b1[:])
            for i in range(2):
                w = nw[:, i * HD:(i + 1) * HD]
                nc.vector.tensor_tensor(out=mcos[:, i], in0=ident[:], in1=w, op=ALU.mult)
                nc.vector.tensor_tensor(out=msin[:, i, 0:64], in0=ident[:, 64:128], in1=w[:, 0:64], op=ALU.mult)
                nc.vector.scalar_tensor_tensor(out=msin[:, i, 64:128], in0=ident[:, 0:64], scalar=-1.0, in1=w[:, 64:128], op0=ALU.mult, op1=ALU.mult)
            nc.vector.scalar_tensor_tensor(out=r1n[:], in0=r1[:], scalar=-1.0 / HID, in1=r1[:], op0=ALU.mult, op1=ALU.mult)

        cst = {}

        def flip_cs(g):
            bank = ps.tile([P, 8, HD], BF16, name="csb", tag="mm", bufs=3)
            for i in range(2):
                for j in range(4):
                    nc.tensor.transpose(bank[:, 4 * i + j], cs[g][:, i, j], ident[:])
            cst[g] = rot.tile([P, 8, HD], BF16, name="cst", tag="cst", bufs=1)
            nc.scalar.copy(out=cst[g][:], in_=bank[:])

        tab = {}

        def tables(g, jp, i):
            t = ps.tile([P, 2, 2, HD], F32, name="tab", tag="tab", bufs=2)
            for jl in range(2):
                nc.tensor.matmul(out=t[:, jl, 0], lhsT=cst[g][:, 2 * jp + jl], rhs=mcos[:, i], start=True, stop=True)
                nc.tensor.matmul(out=t[:, jl, 1], lhsT=cst[g][:, 4 + 2 * jp + jl], rhs=msin[:, i], start=True, stop=True)
            tab[g, jp, i] = t

        ta, tb, tw, tg, s2, rst, s1 = {}, {}, {}, {}, {}, {}, {}
        dz = {}

        def squares(k):
            b = k // NCH
            if k % NCH == 0:
                s1[b] = rot.tile([P, NCH * 8], F32, name="s1", tag="s1", bufs=2)
            u = ut[k]
            for jl in range(2):
                for h in range(HPC):
                    i = (k % NCH) * 8 + jl * HPC + h
                    nc.scalar.activation(out=junk[:, i % 4], in_=u[:, jl, h * HD:(h + 1) * HD], func=ACT.Square, accum_out=s1[b][:, i:i + 1])

        def stats_mean(b, cols):
            if b not in rst:
                rst[b] = (rot.tile([P, NCH * 8], F32, name="r", tag="r", bufs=2), rot.tile([P, NCH * 8], F32, name="r3", tag="r3", bufs=2))
            nc.vector.tensor_scalar(out=s1[b][:, cols], in0=s1[b][:, cols], scalar1=1.0 / HD, scalar2=EPS, op0=ALU.mult, op1=ALU.add)

        def stats_root(b, cols):
            nc.scalar.activation(out=s1[b][:, cols], in_=s1[b][:, cols], func=ACT.Sqrt)

        def stats_r(b, cols):
            r, r3 = rst[b]
            nc.vector.reciprocal(out=r[:, cols], in_=s1[b][:, cols])
            nc.vector.scalar_tensor_tensor(out=r3[:, cols], in0=r[:, cols], scalar=-1.0 / HD, in1=r[:, cols], op0=ALU.mult, op1=ALU.mult)
            nc.vector.tensor_tensor(out=r3[:, cols], in0=r3[:, cols], in1=r[:, cols], op=ALU.mult)

        def heads(ap):
            return ap.rearrange("p j (h d) -> p j h d", d=HD)

        def turn_cos(k):
            g, jp, c = units[k]
            t = tab[g, jp, c // 2]
            ta[k] = rot.tile([P, 2, CH], F32, name="ta", tag="ta", bufs=2)
            nc.vector.tensor_tensor(out=heads(ta[k][:]), in0=heads(gt[k][:]), in1=t[:, :, 0].unsqueeze(2).to_broadcast([P, 2, HPC, HD]), op=ALU.mult)

        def turn_sin(k):
            g, jp, c = units[k]
            t = tab[g, jp, c // 2]
            tb[k] = rot.tile([P, 2, CH], F32, name="tb", tag="tb", bufs=2)
            o, gin = heads(tb[k][:]), heads(gt[k][:])
            for lo, hi in ((slice(0, 64), slice(64, 128)), (slice(64, 128), slice(0, 64))):
                nc.vector.tensor_tensor(out=o[:, :, :, lo], in0=gin[:, :, :, hi], in1=t[:, :, 1, lo].unsqueeze(2).to_broadcast([P, 2, HPC, 64]), op=ALU.mult)

        def turn_add(k):
            tw[k] = rot.tile([P, 2, CH], F32, name="tw", tag="tw", bufs=1)
            eng = nc.gpsimd if ADD_ENGINE == "g" else nc.vector
            eng.tensor_tensor(out=tw[k][:], in0=ta[k][:], in1=tb[k][:], op=ALU.add)

        def scale_r(k):
            r = rst[k // NCH][0]
            tg[k] = rot.tile([P, 2, CH], F32, name="tg", tag="tg", bufs=1)
            for jl in range(2):
                for h in range(HPC):
                    i = (k % NCH) * 8 + jl * HPC + h
                    hs = slice(h * HD, (h + 1) * HD)
                    nc.scalar.activation(out=tg[k][:, jl, hs], in_=tw[k][:, jl, hs], func=ACT.Copy, scale=r[:, i:i + 1])

        def product(k):
            nc.vector.tensor_tensor(out=tb[k][:], in0=tw[k][:], in1=ut[k][:], op=ALU.mult)

        def dots(k):
            s2[k] = rot.tile([P, 8], F32, name="s2", tag="s2", bufs=2)
            for jl in range(2):
                for h in range(HPC):
                    i = jl * HPC + h
                    nc.scalar.activation(out=junk[:, i % 4], in_=tb[k][:, jl, h * HD:(h + 1) * HD], func=ACT.Copy, accum_out=s2[k][:, i:i + 1])

        def slope(k):
            r3 = rst[k // NCH][1]
            i = (k % NCH) * 8
            nc.vector.tensor_tensor(out=s2[k][:], in0=s2[k][:], in1=r3[:, i:i + 8], op=ALU.mult)

        def finish(k, half):
            g, jp, c = units[k]
            if jp == 0 and half == 0:
                dz[g, c] = rot.tile([P, 4, CH], BF16, name="dz", tag="dz", bufs=3)
            u = ut[k]
            for jl in (half,):
                for h in range(HPC):
                    i = jl * HPC + h
                    hs = slice(h * HD, (h + 1) * HD)
                    nc.vector.scalar_tensor_tensor(out=dz[g, c][:, 2 * jp + jl, hs], in0=u[:, jl, hs], scalar=s2[k][:, i:i + 1], in1=tg[k][:, jl, hs], op0=ALU.mult, op1=ALU.add)

        ft = {}
        fbank = {}
        fcodes = {}

        def flip(g, jp, c):
            src = gv[g] if c == NV else dz[g, c]
            bank = ps.tile([P, 2, 2, P], F32, name="tr", tag="tr", bufs=1)
            fbank[g, jp, c] = bank
            for jl in range(2):
                words = src[:, 2 * jp + jl].bitcast(F32)
                for u in range(2):
                    nc.tensor.transpose(bank[:, jl, u], words[:, u:CH // 2:2], ident32[:])

        def flip_copy(g, jp, c):
            bank = fbank[g, jp, c]
            ft[g, jp, c] = rot.tile([P, 2 * P * 4], BF16, name="ft", tag="ft", bufs=2, align_bytes=64)
            nc.scalar.copy(out=ft[g, jp, c][:].bitcast(F32).rearrange("p (j r u) -> p j r u", j=2, u=2), in_=bank[:].rearrange("p j u r -> p j r u"))

        def quantize_flip(g, jp, c):
            fc = rot.tile([P, 2 * P], U32, name="fc", tag="fc", bufs=9, align_bytes=64)
            fs = rot.tile([P, 2 * P], U8, name="fs", tag="fs", bufs=9, align_bytes=64)
            nc.vector.quantize_mx(out=fc[:].bitcast(E5), scales=fs[:], in_=ft[g, jp, c][:])
            fcodes[g, jp, c] = (fc, fs)

        il = {}

        def interleave(g, c, parts=(0, 1)):
            if 0 in parts:
                il[g, c] = rot.tile([P, CH, 4], BF16, name="il", tag="il", bufs=2, align_bytes=64)
            for b in parts:
                cols = slice(b * 256, (b + 1) * 256)
                nc.scalar.copy(out=il[g, c][:, cols].rearrange("p (c i) t -> p c t i", i=4), in_=dz[g, c][:, :, cols].rearrange("p t (c i) -> p c t i", i=4))

        def interleave_pe(dst, src, n0):
            bank = ps.tile([P, 256, 4], BF16, name="ib", tag="mm", bufs=3)
            for b in range(2):
                cols = slice(n0 + b * P, n0 + (b + 1) * P)
                nc.tensor.matmul(out=bank[:, b * P:(b + 1) * P, :], lhsT=ident[:], rhs=src[:, :, cols].rearrange("p j n -> p n j"), start=True, stop=True)
            nc.scalar.copy(out=dst[:, n0:n0 + 256, :], in_=bank[:])

        def interleave_v(g):
            il[g, NV] = rot.tile([P, CH, 4], BF16, name="il", tag="il", bufs=2, align_bytes=64)
            for n0 in (0, 256):
                interleave_pe(il[g, NV], gv[g], n0)

        def quantize_tokens(g, c):
            nc.vector.quantize_mx(out=d_codes[:, g, c].bitcast(E5), scales=d_scales[:, g, c], in_=il[g, c][:].rearrange("p n j -> p (n j)"))

        wil = {}
        hb = {}
        hil = {}

        def interleave_w(kp, bs=(0, 1, 2, 3)):
            if 0 in bs:
                wil[kp] = rot.tile([P, HID, 4], BF16, name="wil", tag="big", bufs=5, align_bytes=64)
            for b in bs:
                interleave_pe(wil[kp], wraw[kp], b * 256)

        def quantize_w(kp):
            nc.vector.quantize_mx(out=w_codes[:, kp].bitcast(E4), scales=w_scales[:, kp], in_=wil[kp][:].rearrange("p n j -> p (n j)"))

        def make_h(g, js):
            if g not in hb:
                hb[g] = rot.tile([P, 4, HID], BF16, name="hb", tag="hb", bufs=1, align_bytes=64)
            for j in js:
                nc.vector.scalar_tensor_tensor(out=hb[g][:, j], in0=xt[g][:, j], scalar=r1[:, 4 * g + j:4 * g + j + 1], in1=lnw[:], op0=ALU.mult, op1=ALU.mult)

        def interleave_h(g, bs=(0, 1, 2, 3)):
            if 0 in bs:
                hil[g] = rot.tile([P, HID, 4], BF16, name="hil", tag="big", bufs=5, align_bytes=64)
            for b in bs:
                cols = slice(b * 256, (b + 1) * 256)
                nc.scalar.copy(out=hil[g][:, cols].rearrange("p (c i) t -> p c t i", i=4), in_=hb[g][:, :, cols].rearrange("p t (c i) -> p c t i", i=4))

        def quantize_h(g):
            nc.vector.quantize_mx(out=h_codes[:, g].bitcast(E4), scales=h_scales[:, g], in_=hil[g][:].rearrange("p n j -> p (n j)"))

        views = (out_1[0:512], out_1[512:1024], out_2, out_3)
        out_rows = out_0.rearrange("(g p j) n -> g j p n", g=2, j=4)

        def input_product(g, j):
            jp, jl = divmod(j, 2)
            banks = []
            for n in range(2):
                bank = ps.tile([P, 512], F32, name="dhb", tag="dh", bufs=2)
                for kp in range(4):
                    fc, fs = fcodes[g, jp, kp]
                    cols = slice(n * 512, (n + 1) * 512)
                    nc.tensor.matmul_mx(
                        out=bank[:], lhsT=fc[:, jl * P:(jl + 1) * P].bitcast(E5), lhsT_scale=fs[:, jl * P:(jl + 1) * P],
                        rhs=w_codes[:, kp, cols].bitcast(E4), rhs_scale=w_scales[:, kp, cols], start=(kp == 0), stop=(kp == 3))
                banks.append(bank)
            return banks

        dhb, gx, sx, wo = {}, {}, {}, {}

        def dh(g, j):
            dhb[g, j] = input_product(g, j)

        def dxa(g, j):
            i = 4 * g + j
            gx[g, j] = rot.tile([P, HID], F32, name="gx", tag="gx", bufs=2)
            sx[g, j] = rot.tile([P, 1], F32, name="sx", tag="sx", bufs=2)
            for n in range(2):
                cols = slice(n * 512, (n + 1) * 512)
                nc.vector.scalar_tensor_tensor(out=gx[g, j][:, cols], in0=dhb[g, j][n][:], scalar=r1[:, i:i + 1], in1=lnw[:, cols], op0=ALU.mult, op1=ALU.mult)

        def dxb(g, j):
            nc.vector.scalar_tensor_tensor(out=junkx[:], in0=gx[g, j][:], scalar=1.0, in1=xt[g][:, j], op0=ALU.mult, op1=ALU.mult, accum_out=sx[g, j][:])

        def dxc(g, j):
            i = 4 * g + j
            nc.vector.tensor_tensor(out=sx[g, j][:], in0=sx[g, j][:], in1=r1n[:, i:i + 1], op=ALU.mult)
            nc.vector.scalar_tensor_tensor(out=gx[g, j][:], in0=xt[g][:, j], scalar=sx[g, j][:], in1=gx[g, j][:], op0=ALU.mult, op1=ALU.add)
            nc.sync.dma_start(out=out_rows[g, j], in_=gx[g, j][:])

        def weight_rows(c, m, engines):
            if m % 2 == 0:
                wo[c] = rot.tile([P, 2, HID], F32, name="wo", tag="big", bufs=5, align_bytes=64)
            o = wo[c][:, m % 2]
            for n in range(2):
                bank = ps.tile([P, 512], F32, name="dwb", tag="mm", bufs=3)
                cols = slice(n * 512, (n + 1) * 512)
                for g in range(2):
                    mc = slice(m * P, (m + 1) * P)
                    nc.tensor.matmul_mx(
                        out=bank[:], lhsT=d_codes[:, g, c, mc].bitcast(E5), lhsT_scale=d_scales[:, g, c, mc],
                        rhs=h_codes[:, g, cols].bitcast(E4), rhs_scale=h_scales[:, g, cols], start=(g == 0), stop=(g == 1))
                if engines[n] == "v":
                    nc.vector.tensor_copy(out=o[:, cols], in_=bank[:])
                else:
                    nc.scalar.copy(out=o[:, cols], in_=bank[:])
            nc.sync.dma_start(out=views[c][m * P:(m + 1) * P], in_=o)


        def whole(f):
            return lambda k: f(*units[k])

        tasks = dict(cos=turn_cos, sin=turn_sin, slope=slope, add=turn_add, fin=finish, flip=whole(flip), scale=scale_r, fcopy=whole(flip_copy),
                     prod=product, dots=dots, qflip=whole(quantize_flip),
                     load_cs=load_cs, load_u=load_u, load_g=load_g, load_x=load_x, load_w=load_w, load_v=load_v, spread=spread_weights, flip_cs=flip_cs, tables=tables,
                     sq=squares, mean=stats_mean, root=stats_root, rr=stats_r, h=make_h, wil=interleave_w, wq=quantize_w, fl=flip, fc=flip_copy, qf=quantize_flip,
                     hil=interleave_h, qh=quantize_h, il=interleave, ilv=interleave_v, qt=quantize_tokens, dh=dh, dxa=dxa, dxb=dxb, dxc=dxc, dw=weight_rows)

        def run(s, slot):
            for name, args in ORDER.get((s, slot), ()):
                tasks[name](*args)

        run(-1, 0)
        for s in range(15):
            for slot, (name, lag, args) in enumerate(CORE):
                if 0 <= s - lag < 12:
                    tasks[name](s - lag, *args)
                run(s, slot)
